import numpy as np
import ml_dtypes


def mxq(x, axis, fmt="e4m3"):
    dtype, down = {"e4m3": (ml_dtypes.float8_e4m3fn, 7), "e5m2": (ml_dtypes.float8_e5m2, 14)}[fmt]
    v = np.moveaxis(np.asarray(x, np.float32).astype(ml_dtypes.bfloat16).astype(np.float64), axis, -1)
    blocks = v.reshape(v.shape[:-1] + (-1, 32))
    amax = np.abs(blocks).max(-1, keepdims=True)
    byte = np.maximum(np.where(amax > 0, np.frexp(amax)[1] - 1 + 127, 0) - down, 1)
    scale = np.exp2(byte - 127.0)
    codes = (blocks / scale).astype(np.float32).astype(dtype).astype(np.float64)
    return np.moveaxis((codes * scale).reshape(v.shape), -1, axis)


WIDE = False


def mx_kscale(k):
    if not WIDE:
        return np.ones(k)
    levels = np.array([10, -10, 5, -5, 0])
    a = np.random.permutation(np.resize(levels, k // 512 * 4)).reshape(k // 512, 4)
    idx = np.arange(k)
    return np.exp2(a[idx // 512, idx % 128 // 32])


BF16 = ml_dtypes.bfloat16


def bf(x):
    return np.asarray(x, np.float32).astype(BF16)


def f64(x):
    return np.asarray(x).astype(np.float64)


T, B, D, M = 16, 64, 1024, 128
TEMP = 0.1
QS = 0.3
SC = 2.0
MS = SC * TEMP / (QS * np.sqrt(D))


def setup_inputs():
    s = mx_kscale(D)
    return {"queries": bf(np.random.standard_normal((T, B, D)) * QS / s),
            "memory_items": bf(np.random.standard_normal((M, D)) * MS * s)}


def reference(queries, memory_items):
    q = f64(queries).reshape(T * B, D)
    mem = f64(memory_items)
    scores = ((mxq(q, 1, "e4m3") @ mxq(mem, 1, "e4m3").T) / TEMP).reshape(T, B, M)
    e = np.exp(scores - scores.max(0, keepdims=True))
    v_att = e / e.sum(0, keepdims=True)
    v = v_att.reshape(T * B, M)
    return (mxq(v, 0, "e4m3").T @ mxq(q, 0, "e4m3")) / B

@@ -1,0 +1,219 @@
+from contextlib import ExitStack
+
+import concourse.mybir as mybir
+from concourse.masks import make_identity
+
+BF16 = mybir.dt.bfloat16
+F32 = mybir.dt.float32
+U32 = mybir.dt.uint32
+U8 = mybir.dt.uint8
+FP8X4 = mybir.dt.float8_e4m3fn_x4
+ALU = mybir.AluOpType
+ACT = mybir.ActivationFunctionType
+AXIS_X = mybir.AxisListType.X
+
+T, B, D, M = 16, 64, 1024, 128
+TEMP = 0.1
+P = 128
+PACK = 4
+K_PASS = P * PACK
+ROWS = T * B
+R_PASSES = ROWS // K_PASS
+D_PASSES = D // K_PASS
+N_TILE = 512
+D_TILES = D // N_TILE
+B_SUB = P // T
+CHUNK = D_PASSES * P
+
+FLOPS = 2 * 2 * ROWS * D * M
+
+
+def tile_gatedmemorymodule_pa_s_kernel(tc, queries, memory_items, out):
+    nc = tc.nc
+    with ExitStack() as ctx:
+        keep = ctx.enter_context(tc.tile_pool(name="keep", bufs=1))
+        soft = ctx.enter_context(tc.tile_pool(name="soft", bufs=R_PASSES))
+        psum_bank = ctx.enter_context(tc.psum_pool(name="psum_bank", bufs=4))
+        psum_scores = ctx.enter_context(tc.psum_pool(name="psum_scores", bufs=R_PASSES))
+        psum_v = ctx.enter_context(tc.psum_pool(name="psum_v", bufs=R_PASSES))
+        ctx.enter_context(tc.manual_schedule())
+
+        ident_f32 = keep.tile([P, P], F32)
+        make_identity(nc, ident_f32[:])
+        ident_bf16 = keep.tile([P, P], BF16)
+        make_identity(nc, ident_bf16[:])
+
+        warm_in = keep.tile([P, 1], F32)
+        warm_out = keep.tile([P, 1], F32)
+        nc.vector.memset(warm_in[:], 0.0)
+        nc.scalar.activation(out=warm_out[:], in_=warm_in[:], func=ACT.Exp)
+
+        mem_sb = keep.tile([P, D], BF16)
+        nc.sync.dma_start(out=mem_sb[:], in_=memory_items)
+        q_view = queries.rearrange("t b d -> (t b) d").rearrange(
+            "(p h l) d -> h l p d", p=P, h=R_PASSES, l=PACK
+        )
+        q_sb = [keep.tile([P, PACK, D], BF16, name="q_sb%d" % h) for h in range(R_PASSES)]
+        for h in range(R_PASSES):
+            for l in range(PACK):
+                nc.sync.dma_start(out=q_sb[h][:, l, :], in_=q_view[h, l, :, :])
+
+        def flip_rows(rows_as_words, grouped_as_words, copy):
+            flipped = psum_bank.tile([P, D_PASSES, 2, P], F32, tag="bank")
+            for g in range(D_PASSES):
+                for u in range(2):
+                    first = (2 * g + u) * P
+                    nc.tensor.transpose(
+                        flipped[:, g, u, :], rows_as_words[:, first : first + P], ident_f32[:]
+                    )
+            copy(
+                out=grouped_as_words.rearrange("p (g r u) -> p g r u", g=D_PASSES, u=2),
+                in_=flipped[:].rearrange("p g u r -> p g r u"),
+            )
+
+        mem_grouped = keep.tile([P, CHUNK * PACK], BF16, align_bytes=64)
+        mem_codes = keep.tile([P, CHUNK], U32, align_bytes=64)
+        mem_scales = keep.tile([P, CHUNK], U8, align_bytes=64)
+        q1_grouped = keep.tile([P, R_PASSES * PACK, CHUNK * PACK], BF16, align_bytes=64)
+        q1_codes = keep.tile([P, R_PASSES * PACK, CHUNK], U32, align_bytes=64)
+        q1_scales = keep.tile([P, R_PASSES * PACK, CHUNK], U8, align_bytes=64)
+        q2_grouped = [
+            keep.tile([P, D, PACK], BF16, name="q2_grouped%d" % h, align_bytes=64)
+            for h in range(R_PASSES)
+        ]
+        q2_codes = keep.tile([P, R_PASSES, D], U32, align_bytes=64)
+        q2_scales = keep.tile([P, R_PASSES, D], U8, align_bytes=64)
+        v_grouped = keep.tile([P, R_PASSES, M, PACK], BF16, align_bytes=64)
+        v_codes = keep.tile([P, R_PASSES, M], U32, align_bytes=64)
+        v_scales = keep.tile([P, R_PASSES, M], U8, align_bytes=64)
+        out_sb = keep.tile([P, D_TILES, N_TILE], F32)
+
+        def score_chunk(h, l, scores):
+            k = h * PACK + l
+            nc.vector.quantize_mx(
+                out=q1_codes[:, k, :].bitcast(FP8X4), scales=q1_scales[:, k, :], in_=q1_grouped[:, k, :]
+            )
+            for g in range(D_PASSES):
+                cols = slice(g * P, (g + 1) * P)
+                nc.tensor.matmul_mx(
+                    out=scores[:, l, :],
+                    lhsT=mem_codes[:, cols].bitcast(FP8X4),
+                    lhsT_scale=mem_scales[:, cols],
+                    rhs=q1_codes[:, k, cols].bitcast(FP8X4),
+                    rhs_scale=q1_scales[:, k, cols],
+                    start=(g == 0),
+                    stop=(g == D_PASSES - 1),
+                )
+
+        def regroup(copy, h, first, width):
+            cols = slice(first, first + width)
+            copy(
+                out=q2_grouped[h][:, cols, :].rearrange("p (a i) l -> p a l i", i=4),
+                in_=q_sb[h][:, :, cols].rearrange("p l (a i) -> p a l i", i=4),
+            )
+
+        def quantise_q2(h, n):
+            cols = slice(n * N_TILE, (n + 1) * N_TILE)
+            nc.vector.quantize_mx(
+                out=q2_codes[:, h, cols].bitcast(FP8X4),
+                scales=q2_scales[:, h, cols],
+                in_=q2_grouped[h][:, cols, :].rearrange("p w l -> p (w l)"),
+            )
+
+        wide = [P, PACK, T, B_SUB]
+
+        def softmax_front(scores):
+            top = soft.tile([P, PACK, B_SUB], F32)
+            nc.vector.tensor_reduce(
+                out=top[:],
+                in_=scores[:].rearrange("m l (t i) -> m l i t", i=B_SUB),
+                axis=AXIS_X,
+                op=ALU.max,
+            )
+            shifted = soft.tile(wide, F32)
+            nc.vector.tensor_tensor(
+                out=shifted[:],
+                in0=scores[:].rearrange("m l (t i) -> m l t i", i=B_SUB),
+                in1=top[:].unsqueeze(2).to_broadcast(wide),
+                op=ALU.subtract,
+            )
+            expd = soft.tile(wide, F32)
+            nc.scalar.activation(out=expd[:], in_=shifted[:], func=ACT.Exp, scale=1.0 / TEMP)
+            return expd
+
+        def softmax_back(h, expd):
+            total = soft.tile([P, PACK, B_SUB], F32)
+            nc.vector.tensor_reduce(
+                out=total[:], in_=expd[:].rearrange("m l t i -> m l i t"), axis=AXIS_X, op=ALU.add
+            )
+            inverse = soft.tile([P, PACK, B_SUB], F32)
+            nc.vector.reciprocal(inverse[:], total[:])
+            v_att = soft.tile(wide, BF16)
+            nc.vector.tensor_tensor(
+                out=v_att[:], in0=expd[:], in1=inverse[:].unsqueeze(2).to_broadcast(wide), op=ALU.mult
+            )
+            v_flipped = psum_v.tile([P, PACK, M], BF16)
+            for l in range(PACK):
+                nc.tensor.transpose(
+                    v_flipped[:, l, :], v_att[:, l, :, :].rearrange("m t i -> m (t i)"), ident_bf16[:]
+                )
+            nc.scalar.copy(out=v_grouped[:, h, :, :], in_=v_flipped[:].rearrange("p l m -> p m l"))
+
+        def pool_pass(h, acc):
+            nc.vector.quantize_mx(
+                out=v_codes[:, h, :].bitcast(FP8X4),
+                scales=v_scales[:, h, :],
+                in_=v_grouped[:, h, :, :].rearrange("p m l -> p (m l)"),
+            )
+            for n in range(D_TILES):
+                cols = slice(n * N_TILE, (n + 1) * N_TILE)
+                nc.tensor.matmul_mx(
+                    out=acc[n][:],
+                    lhsT=v_codes[:, h, :].bitcast(FP8X4),
+                    lhsT_scale=v_scales[:, h, :],
+                    rhs=q2_codes[:, h, cols].bitcast(FP8X4),
+                    rhs_scale=q2_scales[:, h, cols],
+                    start=(h == 0),
+                    stop=(h == R_PASSES - 1),
+                )
+
+        flip_rows(mem_sb[:].bitcast(F32), mem_grouped[:].bitcast(F32), nc.vector.tensor_copy)
+        nc.vector.quantize_mx(
+            out=mem_codes[:].bitcast(FP8X4), scales=mem_scales[:], in_=mem_grouped[:]
+        )
+        for h in range(R_PASSES):
+            for l in range(PACK):
+                flip_rows(
+                    q_sb[h][:].bitcast(F32)[:, l, :],
+                    q1_grouped[:].bitcast(F32)[:, h * PACK + l, :],
+                    nc.scalar.copy,
+                )
+
+        scores = []
+        for h in range(R_PASSES):
+            scores.append(psum_scores.tile([P, PACK, P], F32, name="scores%d" % h, tag="scores"))
+            score_chunk(h, 0, scores[h])
+            score_chunk(h, 1, scores[h])
+            regroup(nc.vector.tensor_copy, h, 0, N_TILE)
+            score_chunk(h, 2, scores[h])
+            score_chunk(h, 3, scores[h])
+            quantise_q2(h, 0)
+
+        HALF = N_TILE // 2
+        regroup(nc.scalar.copy, 0, N_TILE, HALF)
+        regroup(nc.scalar.copy, 0, N_TILE + HALF, HALF)
+        regroup(nc.scalar.copy, 1, N_TILE, HALF)
+        expd = [softmax_front(scores[h]) for h in range(R_PASSES)]
+        regroup(nc.scalar.copy, 1, N_TILE + HALF, HALF)
+        for h in range(R_PASSES):
+            softmax_back(h, expd[h])
+
+        acc = [psum_bank.tile([P, N_TILE], F32, name="acc%d" % n, tag="bank") for n in range(D_TILES)]
+        for h in range(R_PASSES):
+            quantise_q2(h, 1)
+            pool_pass(h, acc)
+
+        nc.scalar.mul(out_sb[:, 0, :], acc[0][:], 1.0 / B)
+        nc.vector.tensor_scalar_mul(out_sb[:, 1, :], acc[1][:], 1.0 / B)
+        for n in range(D_TILES):
+            nc.sync.dma_start(out=out[:, n * N_TILE : (n + 1) * N_TILE], in_=out_sb[:, n, :])

@@ -189,26 +189,30 @@ def tile_gatedmemorymodule_pa_s_kernel(tc, queries, memory_items, out):
                     nc.scalar.copy,
                 )
 
-        scores = []
-        for h in range(R_PASSES):
-            scores.append(psum_scores.tile([P, PACK, P], F32, name="scores%d" % h, tag="scores"))
-            score_chunk(h, 0, scores[h])
-            score_chunk(h, 1, scores[h])
-            regroup(nc.vector.tensor_copy, h, 0, N_TILE)
-            score_chunk(h, 2, scores[h])
-            score_chunk(h, 3, scores[h])
-            quantise_q2(h, 0)
-
         HALF = N_TILE // 2
+        scores = [
+            psum_scores.tile([P, PACK, P], F32, name="scores%d" % h, tag="scores") for h in range(R_PASSES)
+        ]
+        regroup(nc.vector.tensor_copy, 0, 0, N_TILE)
+        for l in range(PACK):
+            score_chunk(0, l, scores[0])
+        quantise_q2(0, 0)
+        regroup(nc.vector.tensor_copy, 1, 0, HALF)
+        for l in range(PACK):
+            score_chunk(1, l, scores[1])
+
         regroup(nc.scalar.copy, 0, N_TILE, HALF)
         regroup(nc.scalar.copy, 0, N_TILE + HALF, HALF)
-        regroup(nc.scalar.copy, 1, N_TILE, HALF)
-        expd = [softmax_front(scores[h]) for h in range(R_PASSES)]
-        regroup(nc.scalar.copy, 1, N_TILE + HALF, HALF)
+        expd = []
+        for h in range(R_PASSES):
+            expd.append(softmax_front(scores[h]))
+            regroup(nc.scalar.copy, 1, N_TILE + h * HALF, HALF)
+        regroup(nc.vector.tensor_copy, 1, HALF, HALF)
         for h in range(R_PASSES):
             softmax_back(h, expd[h])
 
         acc = [psum_bank.tile([P, N_TILE], F32, name="acc%d" % n, tag="bank") for n in range(D_TILES)]
+        quantise_q2(1, 0)
         for h in range(R_PASSES):
             quantise_q2(h, 1)
             pool_pass(h, acc)

@@ -22,6 +22,8 @@ R_PASSES = ROWS // K_PASS
 D_PASSES = D // K_PASS
 N_TILE = 512
 D_TILES = D // N_TILE
+OUT_TILE = 256
+OUT_TILES = D // OUT_TILE
 B_SUB = P // T
 CHUNK = D_PASSES * P
 
@@ -86,7 +88,7 @@ def tile_gatedmemorymodule_pa_s_kernel(tc, queries, memory_items, out):
         v_grouped = keep.tile([P, R_PASSES, M, PACK], BF16, align_bytes=64)
         v_codes = keep.tile([P, R_PASSES, M], U32, align_bytes=64)
         v_scales = keep.tile([P, R_PASSES, M], U8, align_bytes=64)
-        out_sb = keep.tile([P, D_TILES, N_TILE], F32)
+        out_sb = keep.tile([P, OUT_TILES, OUT_TILE], F32)
 
         def score_chunk(h, l, scores):
             k = h * PACK + l
@@ -141,13 +143,19 @@ def tile_gatedmemorymodule_pa_s_kernel(tc, queries, memory_items, out):
             nc.scalar.activation(out=expd[:], in_=shifted[:], func=ACT.Exp, scale=1.0 / TEMP)
             return expd
 
-        def softmax_back(h, expd):
+        def sum_over_t(expd):
             total = soft.tile([P, PACK, B_SUB], F32)
             nc.vector.tensor_reduce(
                 out=total[:], in_=expd[:].rearrange("m l t i -> m l i t"), axis=AXIS_X, op=ALU.add
             )
+            return total
+
+        def invert(total):
             inverse = soft.tile([P, PACK, B_SUB], F32)
             nc.vector.reciprocal(inverse[:], total[:])
+            return inverse
+
+        def normalise_and_flip(h, expd, inverse):
             v_att = soft.tile(wide, BF16)
             nc.vector.tensor_tensor(
                 out=v_att[:], in0=expd[:], in1=inverse[:].unsqueeze(2).to_broadcast(wide), op=ALU.mult
@@ -165,8 +173,8 @@ def tile_gatedmemorymodule_pa_s_kernel(tc, queries, memory_items, out):
                 scales=v_scales[:, h, :],
                 in_=v_grouped[:, h, :, :].rearrange("p m l -> p (m l)"),
             )
-            for n in range(D_TILES):
-                cols = slice(n * N_TILE, (n + 1) * N_TILE)
+            for n in range(OUT_TILES):
+                cols = slice(n * OUT_TILE, (n + 1) * OUT_TILE)
                 nc.tensor.matmul_mx(
                     out=acc[n][:],
                     lhsT=v_codes[:, h, :].bitcast(FP8X4),
@@ -178,9 +186,6 @@ def tile_gatedmemorymodule_pa_s_kernel(tc, queries, memory_items, out):
                 )
 
         flip_rows(mem_sb[:].bitcast(F32), mem_grouped[:].bitcast(F32), nc.vector.tensor_copy)
-        nc.vector.quantize_mx(
-            out=mem_codes[:].bitcast(FP8X4), scales=mem_scales[:], in_=mem_grouped[:]
-        )
         for h in range(R_PASSES):
             for l in range(PACK):
                 flip_rows(
@@ -194,6 +199,9 @@ def tile_gatedmemorymodule_pa_s_kernel(tc, queries, memory_items, out):
             psum_scores.tile([P, PACK, P], F32, name="scores%d" % h, tag="scores") for h in range(R_PASSES)
         ]
         regroup(nc.vector.tensor_copy, 0, 0, N_TILE)
+        nc.vector.quantize_mx(
+            out=mem_codes[:].bitcast(FP8X4), scales=mem_scales[:], in_=mem_grouped[:]
+        )
         for l in range(PACK):
             score_chunk(0, l, scores[0])
         quantise_q2(0, 0)
@@ -203,21 +211,27 @@ def tile_gatedmemorymodule_pa_s_kernel(tc, queries, memory_items, out):
 
         regroup(nc.scalar.copy, 0, N_TILE, HALF)
         regroup(nc.scalar.copy, 0, N_TILE + HALF, HALF)
-        expd = []
-        for h in range(R_PASSES):
-            expd.append(softmax_front(scores[h]))
-            regroup(nc.scalar.copy, 1, N_TILE + h * HALF, HALF)
+        expd = [softmax_front(scores[h]) for h in range(R_PASSES)]
+        regroup(nc.scalar.copy, 1, N_TILE, HALF)
+        regroup(nc.scalar.copy, 1, N_TILE + HALF, HALF)
+        total = [sum_over_t(expd[0])]
         regroup(nc.vector.tensor_copy, 1, HALF, HALF)
+        total.append(sum_over_t(expd[1]))
+        inverse = [invert(total[h]) for h in range(R_PASSES)]
         for h in range(R_PASSES):
-            softmax_back(h, expd[h])
+            normalise_and_flip(h, expd[h], inverse[h])
 
-        acc = [psum_bank.tile([P, N_TILE], F32, name="acc%d" % n, tag="bank") for n in range(D_TILES)]
+        acc = [
+            psum_bank.tile([P, OUT_TILE], F32, name="acc%d" % n, tag="bank") for n in range(OUT_TILES)
+        ]
         quantise_q2(1, 0)
         for h in range(R_PASSES):
             quantise_q2(h, 1)
             pool_pass(h, acc)
 
-        nc.scalar.mul(out_sb[:, 0, :], acc[0][:], 1.0 / B)
-        nc.vector.tensor_scalar_mul(out_sb[:, 1, :], acc[1][:], 1.0 / B)
-        for n in range(D_TILES):
-            nc.sync.dma_start(out=out[:, n * N_TILE : (n + 1) * N_TILE], in_=out_sb[:, n, :])
+        for n in range(OUT_TILES):
+            if n % 2 == 0:
+                nc.scalar.mul(out_sb[:, n, :], acc[n][:], 1.0 / B)
+            else:
+                nc.vector.tensor_scalar_mul(out_sb[:, n, :], acc[n][:], 1.0 / B)
+            nc.sync.dma_start(out=out[:, n * OUT_TILE : (n + 1) * OUT_TILE], in_=out_sb[:, n, :])

@@ -124,7 +124,7 @@ def tile_gatedmemorymodule_pa_s_kernel(tc, queries, memory_items, out):
 
         wide = [P, PACK, T, B_SUB]
 
-        def softmax_front(scores):
+        def max_over_t(scores):
             top = soft.tile([P, PACK, B_SUB], F32)
             nc.vector.tensor_reduce(
                 out=top[:],
@@ -132,6 +132,9 @@ def tile_gatedmemorymodule_pa_s_kernel(tc, queries, memory_items, out):
                 axis=AXIS_X,
                 op=ALU.max,
             )
+            return top
+
+        def exp_shifted(scores, top):
             shifted = soft.tile(wide, F32)
             nc.vector.tensor_tensor(
                 out=shifted[:],
@@ -167,12 +170,14 @@ def tile_gatedmemorymodule_pa_s_kernel(tc, queries, memory_items, out):
                 )
             nc.scalar.copy(out=v_grouped[:, h, :, :], in_=v_flipped[:].rearrange("p l m -> p m l"))
 
-        def pool_pass(h, acc):
+        def quantise_v(h):
             nc.vector.quantize_mx(
                 out=v_codes[:, h, :].bitcast(FP8X4),
                 scales=v_scales[:, h, :],
                 in_=v_grouped[:, h, :, :].rearrange("p m l -> p (m l)"),
             )
+
+        def pool_pass(h, acc):
             for n in range(OUT_TILES):
                 cols = slice(n * OUT_TILE, (n + 1) * OUT_TILE)
                 nc.tensor.matmul_mx(
@@ -194,39 +199,42 @@ def tile_gatedmemorymodule_pa_s_kernel(tc, queries, memory_items, out):
                     nc.scalar.copy,
                 )
 
-        HALF = N_TILE // 2
+        QUARTER = D // 4
         scores = [
             psum_scores.tile([P, PACK, P], F32, name="scores%d" % h, tag="scores") for h in range(R_PASSES)
         ]
-        regroup(nc.vector.tensor_copy, 0, 0, N_TILE)
+        regroup(nc.vector.tensor_copy, 0, 0, 2 * QUARTER)
         nc.vector.quantize_mx(
             out=mem_codes[:].bitcast(FP8X4), scales=mem_scales[:], in_=mem_grouped[:]
         )
         for l in range(PACK):
             score_chunk(0, l, scores[0])
-        quantise_q2(0, 0)
-        regroup(nc.vector.tensor_copy, 1, 0, HALF)
+        regroup(nc.vector.tensor_copy, 1, 0, QUARTER)
         for l in range(PACK):
             score_chunk(1, l, scores[1])
+        quantise_q2(0, 0)
 
-        regroup(nc.scalar.copy, 0, N_TILE, HALF)
-        regroup(nc.scalar.copy, 0, N_TILE + HALF, HALF)
-        expd = [softmax_front(scores[h]) for h in range(R_PASSES)]
-        regroup(nc.scalar.copy, 1, N_TILE, HALF)
-        regroup(nc.scalar.copy, 1, N_TILE + HALF, HALF)
-        total = [sum_over_t(expd[0])]
-        regroup(nc.vector.tensor_copy, 1, HALF, HALF)
-        total.append(sum_over_t(expd[1]))
+        regroup(nc.scalar.copy, 0, 2 * QUARTER, QUARTER)
+        regroup(nc.scalar.copy, 0, 3 * QUARTER, QUARTER)
+        regroup(nc.scalar.copy, 1, QUARTER, QUARTER)
+        top = [max_over_t(scores[h]) for h in range(R_PASSES)]
+        expd = [exp_shifted(scores[h], top[h]) for h in range(R_PASSES)]
+        regroup(nc.scalar.copy, 1, 2 * QUARTER, QUARTER)
+        regroup(nc.scalar.copy, 1, 3 * QUARTER, QUARTER)
+        quantise_q2(0, 1)
+        total = [sum_over_t(expd[h]) for h in range(R_PASSES)]
         inverse = [invert(total[h]) for h in range(R_PASSES)]
         for h in range(R_PASSES):
             normalise_and_flip(h, expd[h], inverse[h])
+        for n in range(D_TILES):
+            quantise_q2(1, n)
 
         acc = [
             psum_bank.tile([P, OUT_TILE], F32, name="acc%d" % n, tag="bank") for n in range(OUT_TILES)
         ]
-        quantise_q2(1, 0)
         for h in range(R_PASSES):
-            quantise_q2(h, 1)
+            quantise_v(h)
+        for h in range(R_PASSES):
             pool_pass(h, acc)
 
         for n in range(OUT_TILES):

@@ -26,6 +26,8 @@ OUT_TILE = 256
 OUT_TILES = D // OUT_TILE
 B_SUB = P // T
 CHUNK = D_PASSES * P
+SPARE_BEFORE_FLIP = 4
+SPARE_BEFORE_POOL = 2
 
 FLOPS = 2 * 2 * ROWS * D * M
 
@@ -190,6 +192,19 @@ def tile_gatedmemorymodule_pa_s_kernel(tc, queries, memory_items, out):
                     stop=(h == R_PASSES - 1),
                 )
 
+        def keep_tensor_engine_busy(spare, passes):
+            cols = slice(N_TILE, 2 * N_TILE)
+            for i in range(passes):
+                nc.tensor.matmul_mx(
+                    out=spare[:],
+                    lhsT=mem_codes[:, 0:P].bitcast(FP8X4),
+                    lhsT_scale=mem_scales[:, 0:P],
+                    rhs=q2_codes[:, 0, cols].bitcast(FP8X4),
+                    rhs_scale=q2_scales[:, 0, cols],
+                    start=True,
+                    stop=True,
+                )
+
         flip_rows(mem_sb[:].bitcast(F32), mem_grouped[:].bitcast(F32), nc.vector.tensor_copy)
         for h in range(R_PASSES):
             for l in range(PACK):
@@ -222,10 +237,13 @@ def tile_gatedmemorymodule_pa_s_kernel(tc, queries, memory_items, out):
         regroup(nc.scalar.copy, 1, 2 * QUARTER, QUARTER)
         regroup(nc.scalar.copy, 1, 3 * QUARTER, QUARTER)
         quantise_q2(0, 1)
+        spare = psum_scores.tile([P, N_TILE], F32, name="spare", tag="scores")
+        keep_tensor_engine_busy(spare, SPARE_BEFORE_FLIP)
         total = [sum_over_t(expd[h]) for h in range(R_PASSES)]
         inverse = [invert(total[h]) for h in range(R_PASSES)]
         for h in range(R_PASSES):
             normalise_and_flip(h, expd[h], inverse[h])
+        keep_tensor_engine_busy(spare, SPARE_BEFORE_POOL)
         for n in range(D_TILES):
             quantise_q2(1, n)
 

@@ -11,6 +11,7 @@ FP8X4 = mybir.dt.float8_e4m3fn_x4
 ALU = mybir.AluOpType
 ACT = mybir.ActivationFunctionType
 AXIS_X = mybir.AxisListType.X
+AXIS_XY = mybir.AxisListType.XY
 
 T, B, D, M = 16, 64, 1024, 128
 TEMP = 0.1
@@ -44,8 +45,6 @@ def tile_gatedmemorymodule_pa_s_kernel(tc, queries, memory_items, out):
 
         ident_f32 = keep.tile([P, P], F32)
         make_identity(nc, ident_f32[:])
-        ident_bf16 = keep.tile([P, P], BF16)
-        make_identity(nc, ident_bf16[:])
 
         warm_in = keep.tile([P, 1], F32)
         warm_out = keep.tile([P, 1], F32)
@@ -124,13 +123,15 @@ def tile_gatedmemorymodule_pa_s_kernel(tc, queries, memory_items, out):
                 in_=q2_grouped[h][:, cols, :].rearrange("p w l -> p (w l)"),
             )
 
-        wide = [P, PACK, T, B_SUB]
+        SLOTS = B_SUB * PACK
+        T_RUN = 4
+        wide = [P, T // T_RUN, SLOTS, T_RUN]
 
         def max_over_t(scores):
-            top = soft.tile([P, PACK, B_SUB], F32)
+            top = soft.tile([P, B_SUB, PACK], F32)
             nc.vector.tensor_reduce(
                 out=top[:],
-                in_=scores[:].rearrange("m l (t i) -> m l i t", i=B_SUB),
+                in_=scores[:].rearrange("m l (t i) -> m i l t", i=B_SUB),
                 axis=AXIS_X,
                 op=ALU.max,
             )
@@ -138,39 +139,48 @@ def tile_gatedmemorymodule_pa_s_kernel(tc, queries, memory_items, out):
 
         def exp_shifted(scores, top):
             shifted = soft.tile(wide, F32)
-            nc.vector.tensor_tensor(
-                out=shifted[:],
-                in0=scores[:].rearrange("m l (t i) -> m l t i", i=B_SUB),
-                in1=top[:].unsqueeze(2).to_broadcast(wide),
-                op=ALU.subtract,
-            )
+            for a in range(T // T_RUN):
+                cols = slice(a * T_RUN * B_SUB, (a + 1) * T_RUN * B_SUB)
+                nc.vector.tensor_tensor(
+                    out=shifted[:, a, :, :].rearrange("m (i l) r -> m i l r", l=PACK),
+                    in0=scores[:, :, cols].rearrange("m l (r i) -> m i l r", i=B_SUB),
+                    in1=top[:].unsqueeze(3).to_broadcast([P, B_SUB, PACK, T_RUN]),
+                    op=ALU.subtract,
+                )
             expd = soft.tile(wide, F32)
             nc.scalar.activation(out=expd[:], in_=shifted[:], func=ACT.Exp, scale=1.0 / TEMP)
             return expd
 
         def sum_over_t(expd):
-            total = soft.tile([P, PACK, B_SUB], F32)
+            total = soft.tile([P, SLOTS], F32)
             nc.vector.tensor_reduce(
-                out=total[:], in_=expd[:].rearrange("m l t i -> m l i t"), axis=AXIS_X, op=ALU.add
+                out=total[:], in_=expd[:].rearrange("m a s r -> m s a r"), axis=AXIS_XY, op=ALU.add
             )
             return total
 
         def invert(total):
-            inverse = soft.tile([P, PACK, B_SUB], F32)
+            inverse = soft.tile([P, SLOTS], F32)
             nc.vector.reciprocal(inverse[:], total[:])
             return inverse
 
         def normalise_and_flip(h, expd, inverse):
-            v_att = soft.tile(wide, BF16)
+            v_att = soft.tile([P, T, SLOTS], BF16)
             nc.vector.tensor_tensor(
-                out=v_att[:], in0=expd[:], in1=inverse[:].unsqueeze(2).to_broadcast(wide), op=ALU.mult
+                out=v_att[:].rearrange("m (a r) s -> m a s r", r=T_RUN),
+                in0=expd[:],
+                in1=inverse[:].unsqueeze(1).unsqueeze(3).to_broadcast(wide),
+                op=ALU.mult,
             )
-            v_flipped = psum_v.tile([P, PACK, M], BF16)
-            for l in range(PACK):
-                nc.tensor.transpose(
-                    v_flipped[:, l, :], v_att[:, l, :, :].rearrange("m t i -> m (t i)"), ident_bf16[:]
-                )
-            nc.scalar.copy(out=v_grouped[:, h, :, :], in_=v_flipped[:].rearrange("p l m -> p m l"))
+            words = v_att[:].rearrange("m t s -> m (t s)").bitcast(F32)
+            v_flipped = psum_v.tile([P, 2, M], F32)
+            for u in range(2):
+                nc.tensor.transpose(v_flipped[:, u, :], words[:, u : 2 * P : 2], ident_f32[:])
+            nc.scalar.copy(
+                out=v_grouped[:, h, :, :].rearrange("p m l -> p (m l)").bitcast(F32).rearrange(
+                    "p (m u) -> p m u", u=2
+                ),
+                in_=v_flipped[:].rearrange("p u m -> p m u"),
+            )
 
         def quantise_v(h):
             nc.vector.quantize_mx(

@@ -22,7 +22,7 @@ ROWS = T * B
 R_PASSES = ROWS // K_PASS
 D_PASSES = D // K_PASS
 N_TILE = 512
-D_TILES = D // N_TILE
+QUARTER = D // 4
 OUT_TILE = 256
 OUT_TILES = D // OUT_TILE
 B_SUB = P // T
@@ -52,14 +52,21 @@ def tile_gatedmemorymodule_pa_s_kernel(tc, queries, memory_items, out):
         nc.scalar.activation(out=warm_out[:], in_=warm_in[:], func=ACT.Exp)
 
         mem_sb = keep.tile([P, D], BF16)
-        nc.sync.dma_start(out=mem_sb[:], in_=memory_items)
         q_view = queries.rearrange("t b d -> (t b) d").rearrange(
-            "(p h l) d -> h l p d", p=P, h=R_PASSES, l=PACK
+            "(p h l) d -> h p l d", p=P, h=R_PASSES, l=PACK
         )
         q_sb = [keep.tile([P, PACK, D], BF16, name="q_sb%d" % h) for h in range(R_PASSES)]
-        for h in range(R_PASSES):
-            for l in range(PACK):
-                nc.sync.dma_start(out=q_sb[h][:, l, :], in_=q_view[h, l, :, :])
+        def load_q(h, first, count):
+            slots = slice(first, first + count)
+            nc.sync.dma_start(out=q_sb[h][:, slots, :], in_=q_view[h, :, slots, :])
+
+        load_q(0, 0, 1)
+        nc.sync.dma_start(out=mem_sb[:], in_=memory_items)
+        load_q(0, 1, 1)
+        for l in range(2, PACK):
+            load_q(0, l, 1)
+        for l in range(PACK):
+            load_q(1, l, 1)
 
         def flip_rows(rows_as_words, grouped_as_words, copy):
             flipped = psum_bank.tile([P, D_PASSES, 2, P], F32, tag="bank")
@@ -91,32 +98,36 @@ def tile_gatedmemorymodule_pa_s_kernel(tc, queries, memory_items, out):
         v_scales = keep.tile([P, R_PASSES, M], U8, align_bytes=64)
         out_sb = keep.tile([P, OUT_TILES, OUT_TILE], F32)
 
-        def score_chunk(h, l, scores):
+        def quantise_q1(h, l):
             k = h * PACK + l
             nc.vector.quantize_mx(
                 out=q1_codes[:, k, :].bitcast(FP8X4), scales=q1_scales[:, k, :], in_=q1_grouped[:, k, :]
             )
-            for g in range(D_PASSES):
-                cols = slice(g * P, (g + 1) * P)
-                nc.tensor.matmul_mx(
-                    out=scores[:, l, :],
-                    lhsT=mem_codes[:, cols].bitcast(FP8X4),
-                    lhsT_scale=mem_scales[:, cols],
-                    rhs=q1_codes[:, k, cols].bitcast(FP8X4),
-                    rhs_scale=q1_scales[:, k, cols],
-                    start=(g == 0),
-                    stop=(g == D_PASSES - 1),
-                )
 
-        def regroup(copy, h, first, width):
-            cols = slice(first, first + width)
+        def score_pass(h):
+            for l in range(PACK):
+                k = h * PACK + l
+                for g in range(D_PASSES):
+                    cols = slice(g * P, (g + 1) * P)
+                    nc.tensor.matmul_mx(
+                        out=scores[h][:, l, :],
+                        lhsT=mem_codes[:, cols].bitcast(FP8X4),
+                        lhsT_scale=mem_scales[:, cols],
+                        rhs=q1_codes[:, k, cols].bitcast(FP8X4),
+                        rhs_scale=q1_scales[:, k, cols],
+                        start=(g == 0),
+                        stop=(g == D_PASSES - 1),
+                    )
+
+        def regroup(copy, h, quarter):
+            cols = slice(quarter * QUARTER, (quarter + 1) * QUARTER)
             copy(
                 out=q2_grouped[h][:, cols, :].rearrange("p (a i) l -> p a l i", i=4),
                 in_=q_sb[h][:, :, cols].rearrange("p l (a i) -> p a l i", i=4),
             )
 
-        def quantise_q2(h, n):
-            cols = slice(n * N_TILE, (n + 1) * N_TILE)
+        def quantise_q2(h, first, width):
+            cols = slice(first, first + width)
             nc.vector.quantize_mx(
                 out=q2_codes[:, h, cols].bitcast(FP8X4),
                 scales=q2_scales[:, h, cols],
@@ -127,26 +138,29 @@ def tile_gatedmemorymodule_pa_s_kernel(tc, queries, memory_items, out):
         T_RUN = 4
         wide = [P, T // T_RUN, SLOTS, T_RUN]
 
-        def max_over_t(scores):
+        def max_over_t(h):
             top = soft.tile([P, B_SUB, PACK], F32)
             nc.vector.tensor_reduce(
                 out=top[:],
-                in_=scores[:].rearrange("m l (t i) -> m i l t", i=B_SUB),
+                in_=scores[h][:].rearrange("m l (t i) -> m i l t", i=B_SUB),
                 axis=AXIS_X,
                 op=ALU.max,
             )
             return top
 
-        def exp_shifted(scores, top):
+        def shift(h, top):
             shifted = soft.tile(wide, F32)
             for a in range(T // T_RUN):
                 cols = slice(a * T_RUN * B_SUB, (a + 1) * T_RUN * B_SUB)
                 nc.vector.tensor_tensor(
                     out=shifted[:, a, :, :].rearrange("m (i l) r -> m i l r", l=PACK),
-                    in0=scores[:, :, cols].rearrange("m l (r i) -> m i l r", i=B_SUB),
+                    in0=scores[h][:, :, cols].rearrange("m l (r i) -> m i l r", i=B_SUB),
                     in1=top[:].unsqueeze(3).to_broadcast([P, B_SUB, PACK, T_RUN]),
                     op=ALU.subtract,
                 )
+            return shifted
+
+        def exponentiate(shifted):
             expd = soft.tile(wide, F32)
             nc.scalar.activation(out=expd[:], in_=shifted[:], func=ACT.Exp, scale=1.0 / TEMP)
             return expd
@@ -163,7 +177,7 @@ def tile_gatedmemorymodule_pa_s_kernel(tc, queries, memory_items, out):
             nc.vector.reciprocal(inverse[:], total[:])
             return inverse
 
-        def normalise_and_flip(h, expd, inverse):
+        def normalise(expd, inverse):
             v_att = soft.tile([P, T, SLOTS], BF16)
             nc.vector.tensor_tensor(
                 out=v_att[:].rearrange("m (a r) s -> m a s r", r=T_RUN),
@@ -171,6 +185,9 @@ def tile_gatedmemorymodule_pa_s_kernel(tc, queries, memory_items, out):
                 in1=inverse[:].unsqueeze(1).unsqueeze(3).to_broadcast(wide),
                 op=ALU.mult,
             )
+            return v_att
+
+        def flip_v(h, v_att):
             words = v_att[:].rearrange("m t s -> m (t s)").bitcast(F32)
             v_flipped = psum_v.tile([P, 2, M], F32)
             for u in range(2):
@@ -189,7 +206,7 @@ def tile_gatedmemorymodule_pa_s_kernel(tc, queries, memory_items, out):
                 in_=v_grouped[:, h, :, :].rearrange("p m l -> p (m l)"),
             )
 
-        def pool_pass(h, acc):
+        def pool_pass(h):
             for n in range(OUT_TILES):
                 cols = slice(n * OUT_TILE, (n + 1) * OUT_TILE)
                 nc.tensor.matmul_mx(
@@ -202,7 +219,7 @@ def tile_gatedmemorymodule_pa_s_kernel(tc, queries, memory_items, out):
                     stop=(h == R_PASSES - 1),
                 )
 
-        def keep_tensor_engine_busy(spare, passes):
+        def keep_tensor_engine_busy(passes):
             cols = slice(N_TILE, 2 * N_TILE)
             for i in range(passes):
                 nc.tensor.matmul_mx(
@@ -215,59 +232,82 @@ def tile_gatedmemorymodule_pa_s_kernel(tc, queries, memory_items, out):
                     stop=True,
                 )
 
-        flip_rows(mem_sb[:].bitcast(F32), mem_grouped[:].bitcast(F32), nc.vector.tensor_copy)
-        for h in range(R_PASSES):
-            for l in range(PACK):
-                flip_rows(
-                    q_sb[h][:].bitcast(F32)[:, l, :],
-                    q1_grouped[:].bitcast(F32)[:, h * PACK + l, :],
-                    nc.scalar.copy,
-                )
-
-        QUARTER = D // 4
         scores = [
             psum_scores.tile([P, PACK, P], F32, name="scores%d" % h, tag="scores") for h in range(R_PASSES)
         ]
-        regroup(nc.vector.tensor_copy, 0, 0, 2 * QUARTER)
+
+        def flip_q(h, l):
+            flip_rows(
+                q_sb[h][:].bitcast(F32)[:, l, :],
+                q1_grouped[:].bitcast(F32)[:, h * PACK + l, :],
+                nc.scalar.copy,
+            )
+
+        on_vector = nc.vector.tensor_copy
+        on_scalar = nc.scalar.copy
+
+        def on_gpsimd(out, in_):
+            nc.gpsimd.tensor_scalar(out, in_, one[:], 0.0, op0=ALU.mult, op1=ALU.add)
+
+        flip_q(0, 0)
+        flip_rows(mem_sb[:].bitcast(F32), mem_grouped[:].bitcast(F32), on_vector)
+        for l in range(1, PACK):
+            flip_q(0, l)
+        for l in range(PACK):
+            flip_q(1, l)
+
+        quantise_q1(0, 0)
         nc.vector.quantize_mx(
             out=mem_codes[:].bitcast(FP8X4), scales=mem_scales[:], in_=mem_grouped[:]
         )
+        regroup(on_vector, 0, 0)
+        quantise_q1(0, 1)
+        quantise_q1(0, 2)
+        regroup(on_vector, 0, 1)
+        quantise_q1(0, 3)
+        score_pass(0)
         for l in range(PACK):
-            score_chunk(0, l, scores[0])
-        regroup(nc.vector.tensor_copy, 1, 0, QUARTER)
-        for l in range(PACK):
-            score_chunk(1, l, scores[1])
-        quantise_q2(0, 0)
+            quantise_q1(1, l)
+        score_pass(1)
+        quantise_q2(0, 0, N_TILE)
 
-        regroup(nc.scalar.copy, 0, 2 * QUARTER, QUARTER)
-        regroup(nc.scalar.copy, 0, 3 * QUARTER, QUARTER)
-        regroup(nc.scalar.copy, 1, QUARTER, QUARTER)
-        top = [max_over_t(scores[h]) for h in range(R_PASSES)]
-        expd = [exp_shifted(scores[h], top[h]) for h in range(R_PASSES)]
-        regroup(nc.scalar.copy, 1, 2 * QUARTER, QUARTER)
-        regroup(nc.scalar.copy, 1, 3 * QUARTER, QUARTER)
-        quantise_q2(0, 1)
+        one = keep.tile([P, 1], F32)
+        nc.vector.memset(one[:], 1.0)
+        regroup(on_gpsimd, 1, 0)
+
+        regroup(on_scalar, 0, 2)
+        regroup(on_scalar, 0, 3)
+        regroup(on_scalar, 1, 1)
+        top = [max_over_t(h) for h in range(R_PASSES)]
+        shifted = [shift(h, top[h]) for h in range(R_PASSES)]
+        expd = [exponentiate(shifted[h]) for h in range(R_PASSES)]
+        regroup(on_scalar, 1, 2)
+        regroup(on_scalar, 1, 3)
+        quantise_q2(0, N_TILE, N_TILE)
         spare = psum_scores.tile([P, N_TILE], F32, name="spare", tag="scores")
-        keep_tensor_engine_busy(spare, SPARE_BEFORE_FLIP)
+        keep_tensor_engine_busy(SPARE_BEFORE_FLIP)
         total = [sum_over_t(expd[h]) for h in range(R_PASSES)]
         inverse = [invert(total[h]) for h in range(R_PASSES)]
+        v_att = [normalise(expd[h], inverse[h]) for h in range(R_PASSES)]
         for h in range(R_PASSES):
-            normalise_and_flip(h, expd[h], inverse[h])
-        keep_tensor_engine_busy(spare, SPARE_BEFORE_POOL)
-        for n in range(D_TILES):
-            quantise_q2(1, n)
+            flip_v(h, v_att[h])
+        keep_tensor_engine_busy(SPARE_BEFORE_POOL)
 
         acc = [
             psum_bank.tile([P, OUT_TILE], F32, name="acc%d" % n, tag="bank") for n in range(OUT_TILES)
         ]
-        for h in range(R_PASSES):
-            quantise_v(h)
-        for h in range(R_PASSES):
-            pool_pass(h, acc)
+        quantise_q2(1, 0, N_TILE)
+        quantise_v(0)
+        pool_pass(0)
+        quantise_q2(1, N_TILE, OUT_TILE)
+        quantise_v(1)
+        quantise_q2(1, N_TILE + OUT_TILE, OUT_TILE)
+        pool_pass(1)
 
-        for n in range(OUT_TILES):
-            if n % 2 == 0:
-                nc.scalar.mul(out_sb[:, n, :], acc[n][:], 1.0 / B)
-            else:
-                nc.vector.tensor_scalar_mul(out_sb[:, n, :], acc[n][:], 1.0 / B)
-            nc.sync.dma_start(out=out[:, n * OUT_TILE : (n + 1) * OUT_TILE], in_=out_sb[:, n, :])
+        for n in range(0, OUT_TILES, 2):
+            nc.scalar.mul(out_sb[:, n, :], acc[n][:], 1.0 / B)
+            nc.vector.tensor_scalar_mul(out_sb[:, n + 1, :], acc[n + 1][:], 1.0 / B)
+            nc.sync.dma_start(
+                out=out[:, n * OUT_TILE : (n + 2) * OUT_TILE],
+                in_=out_sb[:, n : n + 2, :].rearrange("p n w -> p (n w)"),
+            )

@@ -98,10 +98,12 @@ def tile_gatedmemorymodule_pa_s_kernel(tc, queries, memory_items, out):
         v_scales = keep.tile([P, R_PASSES, M], U8, align_bytes=64)
         out_sb = keep.tile([P, OUT_TILES, OUT_TILE], F32)
 
-        def quantise_q1(h, l):
-            k = h * PACK + l
+        def quantise_q1(h, first, count):
+            slots = slice(h * PACK + first, h * PACK + first + count)
             nc.vector.quantize_mx(
-                out=q1_codes[:, k, :].bitcast(FP8X4), scales=q1_scales[:, k, :], in_=q1_grouped[:, k, :]
+                out=q1_codes[:, slots, :].rearrange("p k w -> p (k w)").bitcast(FP8X4),
+                scales=q1_scales[:, slots, :].rearrange("p k w -> p (k w)"),
+                in_=q1_grouped[:, slots, :].rearrange("p k w -> p (k w)"),
             )
 
         def score_pass(h):
@@ -246,39 +248,34 @@ def tile_gatedmemorymodule_pa_s_kernel(tc, queries, memory_items, out):
         on_vector = nc.vector.tensor_copy
         on_scalar = nc.scalar.copy
 
-        def on_gpsimd(out, in_):
-            nc.gpsimd.tensor_scalar(out, in_, one[:], 0.0, op0=ALU.mult, op1=ALU.add)
-
         flip_q(0, 0)
-        flip_rows(mem_sb[:].bitcast(F32), mem_grouped[:].bitcast(F32), on_vector)
+        flip_rows(mem_sb[:].bitcast(F32), mem_grouped[:].bitcast(F32), on_scalar)
         for l in range(1, PACK):
             flip_q(0, l)
         for l in range(PACK):
             flip_q(1, l)
 
-        quantise_q1(0, 0)
+        quantise_q1(0, 0, 1)
+        regroup(on_vector, 0, 0)
         nc.vector.quantize_mx(
             out=mem_codes[:].bitcast(FP8X4), scales=mem_scales[:], in_=mem_grouped[:]
         )
-        regroup(on_vector, 0, 0)
-        quantise_q1(0, 1)
-        quantise_q1(0, 2)
         regroup(on_vector, 0, 1)
-        quantise_q1(0, 3)
+        quantise_q1(0, 1, 2)
+        quantise_q1(0, 3, 1)
         score_pass(0)
-        for l in range(PACK):
-            quantise_q1(1, l)
+        regroup(on_vector, 1, 0)
+        quantise_q1(1, 0, 2)
+        quantise_q1(1, 2, 1)
+        quantise_q1(1, 3, 1)
         score_pass(1)
-        quantise_q2(0, 0, N_TILE)
-
-        one = keep.tile([P, 1], F32)
-        nc.vector.memset(one[:], 1.0)
-        regroup(on_gpsimd, 1, 0)
 
         regroup(on_scalar, 0, 2)
         regroup(on_scalar, 0, 3)
         regroup(on_scalar, 1, 1)
-        top = [max_over_t(h) for h in range(R_PASSES)]
+        top = [max_over_t(0)]
+        quantise_q2(0, 0, N_TILE)
+        top.append(max_over_t(1))
         shifted = [shift(h, top[h]) for h in range(R_PASSES)]
         expd = [exponentiate(shifted[h]) for h in range(R_PASSES)]
         regroup(on_scalar, 1, 2)

@@ -27,6 +27,7 @@ OUT_TILE = 256
 OUT_TILES = D // OUT_TILE
 B_SUB = P // T
 CHUNK = D_PASSES * P
+GPSIMD_COLS = 64
 SPARE_BEFORE_FLIP = 4
 SPARE_BEFORE_POOL = 2
 
@@ -122,7 +123,10 @@ def tile_gatedmemorymodule_pa_s_kernel(tc, queries, memory_items, out):
                     )
 
         def regroup(copy, h, quarter):
-            cols = slice(quarter * QUARTER, (quarter + 1) * QUARTER)
+            regroup_cols(copy, h, quarter * QUARTER, QUARTER)
+
+        def regroup_cols(copy, h, first, width):
+            cols = slice(first, first + width)
             copy(
                 out=q2_grouped[h][:, cols, :].rearrange("p (a i) l -> p a l i", i=4),
                 in_=q_sb[h][:, :, cols].rearrange("p l (a i) -> p a l i", i=4),
@@ -248,6 +252,15 @@ def tile_gatedmemorymodule_pa_s_kernel(tc, queries, memory_items, out):
         on_vector = nc.vector.tensor_copy
         on_scalar = nc.scalar.copy
 
+        def regroup_on_gpsimd(h, first, width):
+            for start in range(first, first + width, GPSIMD_COLS):
+                regroup_cols(
+                    lambda out, in_: nc.gpsimd.tensor_scalar(out, in_, one[:], 0.0, op0=ALU.mult, op1=ALU.add),
+                    h,
+                    start,
+                    GPSIMD_COLS,
+                )
+
         flip_q(0, 0)
         flip_rows(mem_sb[:].bitcast(F32), mem_grouped[:].bitcast(F32), on_scalar)
         for l in range(1, PACK):
@@ -264,22 +277,25 @@ def tile_gatedmemorymodule_pa_s_kernel(tc, queries, memory_items, out):
         quantise_q1(0, 1, 2)
         quantise_q1(0, 3, 1)
         score_pass(0)
-        regroup(on_vector, 1, 0)
+        quantise_q2(0, 0, N_TILE)
         quantise_q1(1, 0, 2)
         quantise_q1(1, 2, 1)
         quantise_q1(1, 3, 1)
         score_pass(1)
 
+        one = keep.tile([P, 1], F32)
+        nc.vector.memset(one[:], 1.0)
+        regroup_on_gpsimd(1, 0, QUARTER)
+        regroup_on_gpsimd(1, D - QUARTER // 2, QUARTER // 2)
+
         regroup(on_scalar, 0, 2)
         regroup(on_scalar, 0, 3)
-        regroup(on_scalar, 1, 1)
-        top = [max_over_t(0)]
-        quantise_q2(0, 0, N_TILE)
-        top.append(max_over_t(1))
+        top = [max_over_t(h) for h in range(R_PASSES)]
         shifted = [shift(h, top[h]) for h in range(R_PASSES)]
         expd = [exponentiate(shifted[h]) for h in range(R_PASSES)]
+        regroup(on_scalar, 1, 1)
         regroup(on_scalar, 1, 2)
-        regroup(on_scalar, 1, 3)
+        regroup_cols(on_scalar, 1, 3 * QUARTER, QUARTER // 2)
         quantise_q2(0, N_TILE, N_TILE)
         spare = psum_scores.tile([P, N_TILE], F32, name="spare", tag="scores")
         keep_tensor_engine_busy(SPARE_BEFORE_FLIP)
@@ -294,11 +310,11 @@ def tile_gatedmemorymodule_pa_s_kernel(tc, queries, memory_items, out):
             psum_bank.tile([P, OUT_TILE], F32, name="acc%d" % n, tag="bank") for n in range(OUT_TILES)
         ]
         quantise_q2(1, 0, N_TILE)
+        quantise_q2(1, N_TILE, OUT_TILE)
         quantise_v(0)
         pool_pass(0)
-        quantise_q2(1, N_TILE, OUT_TILE)
-        quantise_v(1)
         quantise_q2(1, N_TILE + OUT_TILE, OUT_TILE)
+        quantise_v(1)
         pool_pass(1)
 
         for n in range(0, OUT_TILES, 2):

@@ -27,7 +27,7 @@ OUT_TILE = 256
 OUT_TILES = D // OUT_TILE
 B_SUB = P // T
 CHUNK = D_PASSES * P
-GPSIMD_COLS = 64
+GPSIMD_COLS = 128
 SPARE_BEFORE_FLIP = 4
 SPARE_BEFORE_POOL = 2
 

@@ -27,7 +27,6 @@ OUT_TILE = 256
 OUT_TILES = D // OUT_TILE
 B_SUB = P // T
 CHUNK = D_PASSES * P
-GPSIMD_COLS = 128
 SPARE_BEFORE_FLIP = 4
 SPARE_BEFORE_POOL = 2
 
@@ -252,14 +251,8 @@ def tile_gatedmemorymodule_pa_s_kernel(tc, queries, memory_items, out):
         on_vector = nc.vector.tensor_copy
         on_scalar = nc.scalar.copy
 
-        def regroup_on_gpsimd(h, first, width):
-            for start in range(first, first + width, GPSIMD_COLS):
-                regroup_cols(
-                    lambda out, in_: nc.gpsimd.tensor_scalar(out, in_, one[:], 0.0, op0=ALU.mult, op1=ALU.add),
-                    h,
-                    start,
-                    GPSIMD_COLS,
-                )
+        def on_gpsimd(out, in_):
+            nc.gpsimd.tensor_scalar(out, in_, one[:], 0.0, op0=ALU.mult, op1=ALU.add)
 
         flip_q(0, 0)
         flip_rows(mem_sb[:].bitcast(F32), mem_grouped[:].bitcast(F32), on_scalar)
@@ -285,8 +278,8 @@ def tile_gatedmemorymodule_pa_s_kernel(tc, queries, memory_items, out):
 
         one = keep.tile([P, 1], F32)
         nc.vector.memset(one[:], 1.0)
-        regroup_on_gpsimd(1, 0, QUARTER)
-        regroup_on_gpsimd(1, D - QUARTER // 2, QUARTER // 2)
+        regroup_cols(on_gpsimd, 1, 0, QUARTER)
+        regroup_cols(on_gpsimd, 1, D - QUARTER // 2, QUARTER // 2)
 
         regroup(on_scalar, 0, 2)
         regroup(on_scalar, 0, 3)

@@ -27,6 +27,7 @@ OUT_TILE = 256
 OUT_TILES = D // OUT_TILE
 B_SUB = P // T
 CHUNK = D_PASSES * P
+COPY_RUN = 8
 SPARE_BEFORE_FLIP = 4
 SPARE_BEFORE_POOL = 2
 
@@ -127,8 +128,8 @@ def tile_gatedmemorymodule_pa_s_kernel(tc, queries, memory_items, out):
         def regroup_cols(copy, h, first, width):
             cols = slice(first, first + width)
             copy(
-                out=q2_grouped[h][:, cols, :].rearrange("p (a i) l -> p a l i", i=4),
-                in_=q_sb[h][:, :, cols].rearrange("p l (a i) -> p a l i", i=4),
+                out=q2_grouped[h][:, cols, :].rearrange("p (a i) l -> p a l i", i=COPY_RUN),
+                in_=q_sb[h][:, :, cols].rearrange("p l (a i) -> p a l i", i=COPY_RUN),
             )
 
         def quantise_q2(h, first, width):

from contextlib import ExitStack

import concourse.mybir as mybir
from concourse.masks import make_identity

BF16 = mybir.dt.bfloat16
F32 = mybir.dt.float32
U32 = mybir.dt.uint32
U8 = mybir.dt.uint8
FP8X4 = mybir.dt.float8_e4m3fn_x4
ALU = mybir.AluOpType
ACT = mybir.ActivationFunctionType
AXIS_X = mybir.AxisListType.X
AXIS_XY = mybir.AxisListType.XY

T, B, D, M = 16, 64, 1024, 128
TEMP = 0.1
P = 128
PACK = 4
K_PASS = P * PACK
ROWS = T * B
R_PASSES = ROWS // K_PASS
D_PASSES = D // K_PASS
N_TILE = 512
QUARTER = D // 4
OUT_TILE = 256
OUT_TILES = D // OUT_TILE
B_SUB = P // T
CHUNK = D_PASSES * P
COPY_RUN = 8
SPARE_BEFORE_FLIP = 4
SPARE_BEFORE_POOL = 2

FLOPS = 2 * 2 * ROWS * D * M


def tile_gatedmemorymodule_pa_s_kernel(tc, queries, memory_items, out):
    nc = tc.nc
    with ExitStack() as ctx:
        keep = ctx.enter_context(tc.tile_pool(name="keep", bufs=1))
        soft = ctx.enter_context(tc.tile_pool(name="soft", bufs=R_PASSES))
        psum_bank = ctx.enter_context(tc.psum_pool(name="psum_bank", bufs=4))
        psum_scores = ctx.enter_context(tc.psum_pool(name="psum_scores", bufs=R_PASSES))
        psum_v = ctx.enter_context(tc.psum_pool(name="psum_v", bufs=R_PASSES))
        ctx.enter_context(tc.manual_schedule())

        ident_f32 = keep.tile([P, P], F32)
        make_identity(nc, ident_f32[:])

        warm_in = keep.tile([P, 1], F32)
        warm_out = keep.tile([P, 1], F32)
        nc.vector.memset(warm_in[:], 0.0)
        nc.scalar.activation(out=warm_out[:], in_=warm_in[:], func=ACT.Exp)

        mem_sb = keep.tile([P, D], BF16)
        q_view = queries.rearrange("t b d -> (t b) d").rearrange(
            "(p h l) d -> h p l d", p=P, h=R_PASSES, l=PACK
        )
        q_sb = [keep.tile([P, PACK, D], BF16, name="q_sb%d" % h) for h in range(R_PASSES)]
        def load_q(h, first, count):
            slots = slice(first, first + count)
            nc.sync.dma_start(out=q_sb[h][:, slots, :], in_=q_view[h, :, slots, :])

        load_q(0, 0, 1)
        nc.sync.dma_start(out=mem_sb[:], in_=memory_items)
        load_q(0, 1, 1)
        for l in range(2, PACK):
            load_q(0, l, 1)
        for l in range(PACK):
            load_q(1, l, 1)

        def flip_rows(rows_as_words, grouped_as_words, copy):
            flipped = psum_bank.tile([P, D_PASSES, 2, P], F32, tag="bank")
            for g in range(D_PASSES):
                for u in range(2):
                    first = (2 * g + u) * P
                    nc.tensor.transpose(
                        flipped[:, g, u, :], rows_as_words[:, first : first + P], ident_f32[:]
                    )
            copy(
                out=grouped_as_words.rearrange("p (g r u) -> p g r u", g=D_PASSES, u=2),
                in_=flipped[:].rearrange("p g u r -> p g r u"),
            )

        mem_grouped = keep.tile([P, CHUNK * PACK], BF16, align_bytes=64)
        mem_codes = keep.tile([P, CHUNK], U32, align_bytes=64)
        mem_scales = keep.tile([P, CHUNK], U8, align_bytes=64)
        q1_grouped = keep.tile([P, R_PASSES * PACK, CHUNK * PACK], BF16, align_bytes=64)
        q1_codes = keep.tile([P, R_PASSES * PACK, CHUNK], U32, align_bytes=64)
        q1_scales = keep.tile([P, R_PASSES * PACK, CHUNK], U8, align_bytes=64)
        q2_grouped = [
            keep.tile([P, D, PACK], BF16, name="q2_grouped%d" % h, align_bytes=64)
            for h in range(R_PASSES)
        ]
        q2_codes = keep.tile([P, R_PASSES, D], U32, align_bytes=64)
        q2_scales = keep.tile([P, R_PASSES, D], U8, align_bytes=64)
        v_grouped = keep.tile([P, R_PASSES, M, PACK], BF16, align_bytes=64)
        v_codes = keep.tile([P, R_PASSES, M], U32, align_bytes=64)
        v_scales = keep.tile([P, R_PASSES, M], U8, align_bytes=64)
        out_sb = keep.tile([P, OUT_TILES, OUT_TILE], F32)

        def quantise_q1(h, first, count):
            slots = slice(h * PACK + first, h * PACK + first + count)
            nc.vector.quantize_mx(
                out=q1_codes[:, slots, :].rearrange("p k w -> p (k w)").bitcast(FP8X4),
                scales=q1_scales[:, slots, :].rearrange("p k w -> p (k w)"),
                in_=q1_grouped[:, slots, :].rearrange("p k w -> p (k w)"),
            )

        def score_pass(h):
            for l in range(PACK):
                k = h * PACK + l
                for g in range(D_PASSES):
                    cols = slice(g * P, (g + 1) * P)
                    nc.tensor.matmul_mx(
                        out=scores[h][:, l, :],
                        lhsT=mem_codes[:, cols].bitcast(FP8X4),
                        lhsT_scale=mem_scales[:, cols],
                        rhs=q1_codes[:, k, cols].bitcast(FP8X4),
                        rhs_scale=q1_scales[:, k, cols],
                        start=(g == 0),
                        stop=(g == D_PASSES - 1),
                    )

        def regroup(copy, h, quarter):
            regroup_cols(copy, h, quarter * QUARTER, QUARTER)

        def regroup_cols(copy, h, first, width):
            cols = slice(first, first + width)
            copy(
                out=q2_grouped[h][:, cols, :].rearrange("p (a i) l -> p a l i", i=COPY_RUN),
                in_=q_sb[h][:, :, cols].rearrange("p l (a i) -> p a l i", i=COPY_RUN),
            )

        def quantise_q2(h, first, width):
            cols = slice(first, first + width)
            nc.vector.quantize_mx(
                out=q2_codes[:, h, cols].bitcast(FP8X4),
                scales=q2_scales[:, h, cols],
                in_=q2_grouped[h][:, cols, :].rearrange("p w l -> p (w l)"),
            )

        SLOTS = B_SUB * PACK
        T_RUN = 4
        wide = [P, T // T_RUN, SLOTS, T_RUN]

        def max_over_t(h):
            top = soft.tile([P, B_SUB, PACK], F32)
            nc.vector.tensor_reduce(
                out=top[:],
                in_=scores[h][:].rearrange("m l (t i) -> m i l t", i=B_SUB),
                axis=AXIS_X,
                op=ALU.max,
            )
            return top

        def shift(h, top):
            shifted = soft.tile(wide, F32)
            for a in range(T // T_RUN):
                cols = slice(a * T_RUN * B_SUB, (a + 1) * T_RUN * B_SUB)
                nc.vector.tensor_tensor(
                    out=shifted[:, a, :, :].rearrange("m (i l) r -> m i l r", l=PACK),
                    in0=scores[h][:, :, cols].rearrange("m l (r i) -> m i l r", i=B_SUB),
                    in1=top[:].unsqueeze(3).to_broadcast([P, B_SUB, PACK, T_RUN]),
                    op=ALU.subtract,
                )
            return shifted

        def exponentiate(shifted):
            expd = soft.tile(wide, F32)
            nc.scalar.activation(out=expd[:], in_=shifted[:], func=ACT.Exp, scale=1.0 / TEMP)
            return expd

        def sum_over_t(expd):
            total = soft.tile([P, SLOTS], F32)
            nc.vector.tensor_reduce(
                out=total[:], in_=expd[:].rearrange("m a s r -> m s a r"), axis=AXIS_XY, op=ALU.add
            )
            return total

        def invert(total):
            inverse = soft.tile([P, SLOTS], F32)
            nc.vector.reciprocal(inverse[:], total[:])
            return inverse

        def normalise(expd, inverse):
            v_att = soft.tile([P, T, SLOTS], BF16)
            nc.vector.tensor_tensor(
                out=v_att[:].rearrange("m (a r) s -> m a s r", r=T_RUN),
                in0=expd[:],
                in1=inverse[:].unsqueeze(1).unsqueeze(3).to_broadcast(wide),
                op=ALU.mult,
            )
            return v_att

        def flip_v(h, v_att):
            words = v_att[:].rearrange("m t s -> m (t s)").bitcast(F32)
            v_flipped = psum_v.tile([P, 2, M], F32)
            for u in range(2):
                nc.tensor.transpose(v_flipped[:, u, :], words[:, u : 2 * P : 2], ident_f32[:])
            nc.scalar.copy(
                out=v_grouped[:, h, :, :].rearrange("p m l -> p (m l)").bitcast(F32).rearrange(
                    "p (m u) -> p m u", u=2
                ),
                in_=v_flipped[:].rearrange("p u m -> p m u"),
            )

        def quantise_v(h):
            nc.vector.quantize_mx(
                out=v_codes[:, h, :].bitcast(FP8X4),
                scales=v_scales[:, h, :],
                in_=v_grouped[:, h, :, :].rearrange("p m l -> p (m l)"),
            )

        def pool_pass(h):
            for n in range(OUT_TILES):
                cols = slice(n * OUT_TILE, (n + 1) * OUT_TILE)
                nc.tensor.matmul_mx(
                    out=acc[n][:],
                    lhsT=v_codes[:, h, :].bitcast(FP8X4),
                    lhsT_scale=v_scales[:, h, :],
                    rhs=q2_codes[:, h, cols].bitcast(FP8X4),
                    rhs_scale=q2_scales[:, h, cols],
                    start=(h == 0),
                    stop=(h == R_PASSES - 1),
                )

        def keep_tensor_engine_busy(passes):
            cols = slice(N_TILE, 2 * N_TILE)
            for i in range(passes):
                nc.tensor.matmul_mx(
                    out=spare[:],
                    lhsT=mem_codes[:, 0:P].bitcast(FP8X4),
                    lhsT_scale=mem_scales[:, 0:P],
                    rhs=q2_codes[:, 0, cols].bitcast(FP8X4),
                    rhs_scale=q2_scales[:, 0, cols],
                    start=True,
                    stop=True,
                )

        scores = [
            psum_scores.tile([P, PACK, P], F32, name="scores%d" % h, tag="scores") for h in range(R_PASSES)
        ]

        def flip_q(h, l):
            flip_rows(
                q_sb[h][:].bitcast(F32)[:, l, :],
                q1_grouped[:].bitcast(F32)[:, h * PACK + l, :],
                nc.scalar.copy,
            )

        on_vector = nc.vector.tensor_copy
        on_scalar = nc.scalar.copy

        def on_gpsimd(out, in_):
            nc.gpsimd.tensor_scalar(out, in_, one[:], 0.0, op0=ALU.mult, op1=ALU.add)

        flip_q(0, 0)
        flip_rows(mem_sb[:].bitcast(F32), mem_grouped[:].bitcast(F32), on_scalar)
        for l in range(1, PACK):
            flip_q(0, l)
        for l in range(PACK):
            flip_q(1, l)

        quantise_q1(0, 0, 1)
        regroup(on_vector, 0, 0)
        nc.vector.quantize_mx(
            out=mem_codes[:].bitcast(FP8X4), scales=mem_scales[:], in_=mem_grouped[:]
        )
        regroup(on_vector, 0, 1)
        quantise_q1(0, 1, 2)
        quantise_q1(0, 3, 1)
        score_pass(0)
        quantise_q2(0, 0, N_TILE)
        quantise_q1(1, 0, 2)
        quantise_q1(1, 2, 1)
        quantise_q1(1, 3, 1)
        score_pass(1)

        one = keep.tile([P, 1], F32)
        nc.vector.memset(one[:], 1.0)
        regroup_cols(on_gpsimd, 1, 0, QUARTER)
        regroup_cols(on_gpsimd, 1, D - QUARTER // 2, QUARTER // 2)

        regroup(on_scalar, 0, 2)
        regroup(on_scalar, 0, 3)
        top = [max_over_t(h) for h in range(R_PASSES)]
        shifted = [shift(h, top[h]) for h in range(R_PASSES)]
        expd = [exponentiate(shifted[h]) for h in range(R_PASSES)]
        regroup(on_scalar, 1, 1)
        regroup(on_scalar, 1, 2)
        regroup_cols(on_scalar, 1, 3 * QUARTER, QUARTER // 2)
        quantise_q2(0, N_TILE, N_TILE)
        spare = psum_scores.tile([P, N_TILE], F32, name="spare", tag="scores")
        keep_tensor_engine_busy(SPARE_BEFORE_FLIP)
        total = [sum_over_t(expd[h]) for h in range(R_PASSES)]
        inverse = [invert(total[h]) for h in range(R_PASSES)]
        v_att = [normalise(expd[h], inverse[h]) for h in range(R_PASSES)]
        for h in range(R_PASSES):
            flip_v(h, v_att[h])
        keep_tensor_engine_busy(SPARE_BEFORE_POOL)

        acc = [
            psum_bank.tile([P, OUT_TILE], F32, name="acc%d" % n, tag="bank") for n in range(OUT_TILES)
        ]
        quantise_q2(1, 0, N_TILE)
        quantise_q2(1, N_TILE, OUT_TILE)
        quantise_v(0)
        pool_pass(0)
        quantise_q2(1, N_TILE + OUT_TILE, OUT_TILE)
        quantise_v(1)
        pool_pass(1)

        for n in range(0, OUT_TILES, 2):
            nc.scalar.mul(out_sb[:, n, :], acc[n][:], 1.0 / B)
            nc.vector.tensor_scalar_mul(out_sb[:, n + 1, :], acc[n + 1][:], 1.0 / B)
            nc.sync.dma_start(
                out=out[:, n * OUT_TILE : (n + 2) * OUT_TILE],
                in_=out_sb[:, n : n + 2, :].rearrange("p n w -> p (n w)"),
            )
